import numpy as np
import ml_dtypes


def mxq(x, axis, fmt="e4m3"):
    dtype, down = {"e4m3": (ml_dtypes.float8_e4m3fn, 7), "e5m2": (ml_dtypes.float8_e5m2, 14)}[fmt]
    v = np.moveaxis(np.asarray(x, np.float32).astype(ml_dtypes.bfloat16).astype(np.float64), axis, -1)
    blocks = v.reshape(v.shape[:-1] + (-1, 32))
    amax = np.abs(blocks).max(-1, keepdims=True)
    byte = np.maximum(np.where(amax > 0, np.frexp(amax)[1] - 1 + 127, 0) - down, 1)
    scale = np.exp2(byte - 127.0)
    codes = (blocks / scale).astype(np.float32).astype(dtype).astype(np.float64)
    return np.moveaxis((codes * scale).reshape(v.shape), -1, axis)


WIDE = False


def mx_kscale(k):
    if not WIDE:
        return np.ones(k)
    levels = np.array([10, -10, 5, -5, 0])
    if k % 512:
        return np.exp2(np.random.permutation(np.resize(levels, k // 32))).repeat(32)
    a = np.empty((k // 512, 16))
    for p in range(k // 512):
        a[p, :8] = np.random.permutation(np.resize(levels, 8))
        for g in range(8):
            far = levels[np.abs(levels - a[p, g]) >= 10]
            a[p, g + 8] = far[np.random.randint(len(far))]
    return np.exp2(a.ravel()).repeat(32)


BF16 = ml_dtypes.bfloat16


def bf(x):
    return np.asarray(x, np.float32).astype(BF16)


def f64(x):
    return np.asarray(x).astype(np.float64)


B, S_IMG, S_TXT, D, H, HD = 1, 768, 256, 1536, 12, 128
S = S_TXT + S_IMG
E = H * HD
EPS = 1e-5


def rmsnorm(x, w):
    var = np.mean(np.square(x), axis=-1, keepdims=True)
    return x * (1.0 / np.sqrt(var + EPS)) * w


def rope(x, cos, sin):
    xr = x.reshape(x.shape[:-1] + (HD // 2, 2))
    x_rot = np.stack([-xr[..., 1], xr[..., 0]], axis=-1).reshape(x.shape)
    return x * cos[None, :, None, :] + x_rot * sin[None, :, None, :]


def draw0():
    r = np.random.standard_normal
    s, u = mx_kscale(D), mx_kscale(D)
    pw = 0.015 / np.sqrt(D)
    return {"hidden_states": bf(r((B, S_IMG, D)) * s),
            "encoder_hidden_states": bf(r((B, S_TXT, D)) * u),
            "rope_cos": bf(np.random.uniform(size=(S, HD))),
            "rope_sin": bf(np.random.uniform(size=(S, HD))),
            "Wq": bf(r((E, D)) * pw / s),
            "Wk": bf(r((E, D)) * pw / s),
            "Waq": bf(r((E, D)) * pw / u),
            "baq": bf(r(E) * 0.005),
            "Wak": bf(r((E, D)) * pw / u),
            "bak": bf(r(E) * 0.005),
            "wq_norm": bf(1.75 + 0.15 * r(HD)),
            "wk_norm": bf(1.75 + 0.15 * r(HD)),
            "waq_norm": bf(1.75 + 0.15 * r(HD)),
            "wak_norm": bf(1.75 + 0.15 * r(HD))}


def core(hidden_states, encoder_hidden_states, rope_cos, rope_sin, Wq, Wk, Waq, baq, Wak, bak, wq_norm, wk_norm, waq_norm, wak_norm):
    xq = mxq(f64(hidden_states), 2, "e4m3")
    cq = mxq(f64(encoder_hidden_states), 2, "e4m3")
    q = (xq @ mxq(f64(Wq).T, 0, "e4m3")).reshape(B, S_IMG, H, HD)
    k = (xq @ mxq(f64(Wk).T, 0, "e4m3")).reshape(B, S_IMG, H, HD)
    q = rmsnorm(q, f64(wq_norm))
    k = rmsnorm(k, f64(wk_norm))
    eq = ((cq @ mxq(f64(Waq).T, 0, "e4m3")) + f64(baq)).reshape(B, S_TXT, H, HD)
    ek = ((cq @ mxq(f64(Wak).T, 0, "e4m3")) + f64(bak)).reshape(B, S_TXT, H, HD)
    eq = rmsnorm(eq, f64(waq_norm))
    ek = rmsnorm(ek, f64(wak_norm))
    q = np.concatenate([eq, q], axis=1)
    k = np.concatenate([ek, k], axis=1)
    return rope(q, f64(rope_cos), f64(rope_sin)), rope(k, f64(rope_cos), f64(rope_sin))


def e4m3fn_bytes(y):
    return np.clip(np.asarray(y, np.float64), -448.0, 448.0).astype(np.float32).astype(ml_dtypes.float8_e4m3fn).view(np.uint8)


def e4m3fn_values(b):
    return np.asarray(b, np.uint8).view(ml_dtypes.float8_e4m3fn).astype(np.float64)


def setup_inputs():
    d = draw0()
    x0 = np.asarray(d['Wq']).astype(np.float64)
    s = (np.max(np.abs(x0), axis=(0,), keepdims=True) / 448.0).astype(np.float32)
    out = {}
    for k, v in d.items():
        if k == 'Wq':
            out['Wq_bytes'] = e4m3fn_bytes(x0 / s.astype(np.float64))
            out['Wq_scale'] = s
        else:
            out[k] = v
    return out


def reference(hidden_states, encoder_hidden_states, rope_cos, rope_sin, Wq_bytes, Wq_scale, Wk, Waq, baq, Wak, bak, wq_norm, wk_norm, waq_norm, wak_norm):
    return core(hidden_states, encoder_hidden_states, rope_cos, rope_sin, e4m3fn_values(Wq_bytes) * Wq_scale.astype(np.float64), Wk, Waq, baq, Wak, bak, wq_norm, wk_norm, waq_norm, wak_norm)

@@ -1,0 +1,371 @@
+from contextlib import ExitStack
+
+import concourse.mybir as mybir
+from concourse.masks import make_identity
+
+F32 = mybir.dt.float32
+BF16 = mybir.dt.bfloat16
+U32 = mybir.dt.uint32
+U8 = mybir.dt.uint8
+FP8 = mybir.dt.float8_e4m3fn
+FP8X4 = mybir.dt.float8_e4m3fn_x4
+MULT = mybir.AluOpType.mult
+ADD = mybir.AluOpType.add
+ACT = mybir.ActivationFunctionType
+ENG = mybir.EngineType
+
+P = 128
+D = 1536
+HD = 128
+PASSES = 3
+CH = 512
+EPS = 1e-5
+FLOPS = 2 * 1024 * 1536 * 3072
+
+RAW_BUFS = 3
+RSQRT = True
+DELAY = 2
+QLAG = 1
+ADD_SPLIT = 1
+LEAD = 3.0
+XLEAD = 1.0
+RMAX = 2.0
+QSP = 3.0
+PIN = (ENG.PE,)
+PERIOD = 2
+DUMMY = False
+CHUNKS = (("q", 0), ("k", 0), ("aq", 0), ("k", 1), ("ak", 0), ("q", 1), ("aq", 1), ("k", 2), ("ak", 1), ("aq", 2), ("ak", 2), ("q", 2))
+
+
+def tile_flux2attention_pa_kernel(
+    tc, hidden_states, encoder_hidden_states, rope_cos, rope_sin, Wq_bytes, Wq_scale, Wk, Waq, baq, Wak, bak,
+    wq_norm, wk_norm, waq_norm, wak_norm, out_0, out_1,
+):
+    nc = tc.nc
+    hid = hidden_states.flatten_outer_dims()
+    enc = encoder_hidden_states.flatten_outer_dims()
+    out_q = out_0.rearrange("b s h d -> (b s) (h d)")
+    out_k = out_1.rearrange("b s h d -> (b s) (h d)")
+    dest = {"q": out_q, "aq": out_q, "k": out_k, "ak": out_k}
+    weight = {"k": Wk, "aq": Waq, "ak": Wak}
+    gain = {"q": wq_norm, "k": wk_norm, "aq": waq_norm, "ak": wak_norm}
+    bias = {"aq": baq, "ak": bak}
+    tiles_of = {"q": (2, 8), "k": (2, 8), "aq": (0, 2), "ak": (0, 2)}
+    names = ("q", "k", "aq", "ak")
+    groups = [("x", i) for i in range(4)] + list(CHUNKS)
+
+    with ExitStack() as ctx:
+        const = ctx.enter_context(tc.tile_pool(name="const", bufs=1))
+        rawp = ctx.enter_context(tc.tile_pool(name="rawp", bufs=RAW_BUFS))
+        grp = ctx.enter_context(tc.tile_pool(name="grp", bufs=4))
+        wcp = ctx.enter_context(tc.tile_pool(name="wcp", bufs=4))
+        epi = ctx.enter_context(tc.tile_pool(name="epi", bufs=4))
+        stat = ctx.enter_context(tc.tile_pool(name="stat", bufs=8))
+        ptp = ctx.enter_context(tc.psum_pool(name="ptp", bufs=4))
+        pmp = ctx.enter_context(tc.psum_pool(name="pmp", bufs=4))
+
+        ident = const.tile([P, P], F32, name="ident")
+        make_identity(nc, ident[:])
+        warm = const.tile([P, 1], F32, name="warm")
+        nc.vector.memset(warm[:], 1.0)
+
+        sq = const.tile([P, PASSES, 4], F32, name="sq")
+        byt = [const.tile([P, 4, D], U8, name="byt%d" % c) for c in range(3)]
+        cos_sb = const.tile([P, 8, HD], BF16, name="cos_sb")
+        sin_sb = const.tile([P, 8, HD], BF16, name="sin_sb")
+        g_bc = const.tile([P, 4, HD], BF16, name="g_bc")
+        gsw = const.tile([P, 4, HD], BF16, name="gsw")
+        b_col = {w: const.tile([P, 12], BF16, name="b_col_" + w) for w in ("aq", "ak")}
+        tab_a = {w: const.tile([P, tiles_of[w][1] - tiles_of[w][0], HD], F32, name="tab_a_" + w) for w in names}
+        tab_b = {w: const.tile([P, tiles_of[w][1] - tiles_of[w][0], HD], F32, name="tab_b_" + w) for w in names}
+        xc = const.tile([P, PASSES, 1024], U32, name="xc", align_bytes=64)
+        xs = const.tile([P, PASSES, 1024], U8, name="xs", align_bytes=64)
+
+        zeros = const.tile([P, CH], BF16, name="zeros")
+        nc.gpsimd.memset(zeros[:], 0.0)
+        count = {"units": 0}
+        raw_of = {}
+        codes_of = {}
+        gr_of = {}
+        xbt_of = {}
+        casts = []
+        live = {}
+
+        def token_rows(src):
+            return src[0:256, :].rearrange("(p j) n -> p j n", j=2)
+
+        def rows(src, r0, n):
+            return src[r0 : r0 + n * P, :].rearrange("(j p) k -> p j k", p=P)
+
+        def load_bytes(c):
+            for half in range(2):
+                nc.sync.dma_start(out=byt[c][:, 2 * half : 2 * half + 2, :], in_=rows(Wq_bytes, c * CH + 256 * half, 2))
+
+        def load_group(gi):
+            kind, c = groups[gi]
+            if kind == "x":
+                raw = rawp.tile([P, 2, D], BF16, name="rawx", bufs=4)
+                nc.sync.dma_start(out=raw[:], in_=(enc.rearrange("(p j) k -> p j k", j=2) if c == 0 else hid.rearrange("(p j) k -> p j k", j=6)[:, 2 * c - 2 : 2 * c, :]))
+            elif kind == "q":
+                raw = rawp.tile([P, 4, D], BF16, name="rawq", bufs=1)
+                casts.extend([(gi, j) for j in range(4)])
+            else:
+                raw = rawp.tile([P, 4, D], BF16, name="raw")
+                nc.sync.dma_start(out=raw[:], in_=rows(weight[kind], c * CH, 4))
+            raw_of[gi] = raw
+
+        def cast(on_vector):
+            gi, j = casts.pop(0)
+            src = byt[groups[gi][1]][:, j, :].bitcast(FP8)
+            if on_vector:
+                nc.vector.tensor_copy(out=raw_of[gi][:, j, :], in_=src)
+            else:
+                nc.scalar.copy(out=raw_of[gi][:, j, :], in_=src)
+
+        def unit(gi, g, half):
+            kind, c = groups[gi]
+            words = raw_of[gi][:].rearrange("p j k -> p (j k)").bitcast(F32)
+            if (gi, g) not in gr_of:
+                if kind == "x":
+                    gr_of[(gi, g)] = grp.tile([P, 1024], BF16, name="grx", align_bytes=64)
+                elif kind == "q":
+                    gr_of[(gi, g)] = grp.tile([P, CH * 4], BF16, name="grq", align_bytes=64, bufs=3)
+                else:
+                    gr_of[(gi, g)] = grp.tile([P, CH * 4], BF16, name="gr", align_bytes=64)
+            gr = gr_of[(gi, g)]
+            pt = ptp.tile([P, 2, 256], F32, name="pt")
+            count["units"] += 1
+            if count["units"] % 3 != 0 and DUMMY:
+                nc.tensor.matmul(out=pt[:].rearrange("p u n -> p (u n)"), lhsT=zeros[:, 0:P], rhs=zeros[:], start=True, stop=True)
+            for jj in range(2):
+                base = (2 * half + jj) * (D // 2) + 256 * g
+                for u in range(2):
+                    nc.tensor.transpose(pt[:, u, jj * P : (jj + 1) * P], words[:, base + u : base + 256 : 2], ident[:])
+            if kind == "q":
+                return lambda: nc.vector.tensor_tensor(
+                    out=gr[:, half * 1024 : (half + 1) * 1024].rearrange("p (n u e) -> p n u e", u=2, e=2),
+                    in0=pt[:].rearrange("p u n -> p (u n)").bitcast(BF16).rearrange("p (u n e) -> p n u e", u=2, e=2),
+                    in1=sq[:, g, :].rearrange("p (o u e) -> p o u e", o=1, u=2).to_broadcast([P, 256, 2, 2]),
+                    op=MULT,
+                )
+            else:
+                gr_words = gr[:].bitcast(F32).rearrange("p (n u) -> p n u", u=2)
+                nc.scalar.copy(out=gr_words[:, half * 256 : (half + 1) * 256, :], in_=pt[:].rearrange("p u n -> p n u"))
+            return None
+
+        def quant(gi, g):
+            kind, c = groups[gi]
+            if kind == "x":
+                codes = xc[:, g, c * 256 : (c + 1) * 256]
+                scales = xs[:, g, c * 256 : (c + 1) * 256]
+            else:
+                if gi not in codes_of:
+                    wc = wcp.tile([P, PASSES, CH], U32, name="wc", align_bytes=64)
+                    ws = wcp.tile([P, PASSES, CH], U8, name="ws", align_bytes=64)
+                    codes_of[gi] = (wc, ws)
+                wc, ws = codes_of[gi]
+                codes = wc[:, g, :]
+                scales = ws[:, g, :]
+            nc.vector.quantize_mx(out=codes.bitcast(FP8X4), scales=scales, in_=gr_of[(gi, g)][:])
+
+        def text_heads(gi):
+            w, c = groups[gi]
+            wc, ws = codes_of[gi]
+            xbt = epi.tile([P, 4, 256], F32, name="xbt", bufs=2)
+            xbt_of[gi] = xbt
+            for hp in range(2):
+                pt = ptp.tile([P, 2, 256], F32, name="pt")
+                for hh in range(2):
+                    cols = slice((2 * hp + hh) * HD, (2 * hp + hh + 1) * HD)
+                    for g in range(PASSES):
+                        nc.tensor.matmul_mx(
+                            out=pt[:, hh, :],
+                            lhsT=wc[:, g, cols].bitcast(FP8X4),
+                            lhsT_scale=ws[:, g, cols],
+                            rhs=xc[:, g, 0:256].bitcast(FP8X4),
+                            rhs_scale=xs[:, g, 0:256],
+                            start=(g == 0),
+                            stop=(g == PASSES - 1),
+                        )
+                for hh in range(2):
+                    h = 2 * hp + hh
+                    nc.scalar.activation(out=xbt[:, h, :], in_=pt[:, hh, :], func=ACT.Identity, bias=b_col[w][:, 4 * c + h : 4 * c + h + 1])
+
+        def bank_a(gi, m):
+            w, c = groups[gi]
+            ps = pmp.tile([P, CH], F32, name="ps")
+            if w in bias:
+                for h in range(4):
+                    nc.tensor.transpose(ps[:, h * HD : (h + 1) * HD], xbt_of[gi][:, h, m * P : (m + 1) * P], ident[:])
+            else:
+                wc, ws = codes_of[gi]
+                for g in range(PASSES):
+                    nc.tensor.matmul_mx(
+                        out=ps[:],
+                        lhsT=xc[:, g, m * P : (m + 1) * P].bitcast(FP8X4),
+                        lhsT_scale=xs[:, g, m * P : (m + 1) * P],
+                        rhs=wc[:, g, :].bitcast(FP8X4),
+                        rhs_scale=ws[:, g, :],
+                        start=(g == 0),
+                        stop=(g == PASSES - 1),
+                    )
+            ss = stat.tile([P, 4], F32, name="ss")
+            r = stat.tile([P, 4], F32, name="r")
+            for h in range(4):
+                junk = epi.tile([P, HD], BF16, name="junk")
+                nc.scalar.activation(out=junk[:], in_=ps[:, h * HD : (h + 1) * HD], func=ACT.Square, accum_out=ss[:, h : h + 1])
+            if RSQRT:
+                nc.scalar.activation(out=r[:], in_=ss[:], func=ACT.Abs_reciprocal_sqrt, scale=1.0 / HD, bias=EPS)
+            else:
+                rt = stat.tile([P, 4], F32, name="rt")
+                nc.scalar.activation(out=rt[:], in_=ss[:], func=ACT.Sqrt, scale=1.0 / HD, bias=EPS)
+                nc.vector.reciprocal(out=r[:], in_=rt[:])
+            live[(gi, m)] = (ps, r)
+
+        def bank_b(gi, m, before_last):
+            w, c = groups[gi]
+            m0 = tiles_of[w][0]
+            x, r = live.pop((gi, m))
+            t1 = epi.tile([P, CH], F32, name="t1")
+            t2 = epi.tile([P, CH], F32, name="t2")
+            o = epi.tile([P, CH], F32, name="o")
+            for h in range(4):
+                cols = slice(h * HD, (h + 1) * HD)
+                nc.vector.scalar_tensor_tensor(out=t1[:, cols], in0=x[:, cols], scalar=r[:, h : h + 1], in1=tab_a[w][:, m - m0, :], op0=MULT, op1=MULT)
+                if h == 3:
+                    before_last()
+                nc.vector.scalar_tensor_tensor(
+                    out=t2[:, cols].rearrange("p (i e) -> p i e", e=2),
+                    in0=x[:, cols].rearrange("p (i e) -> p i e", e=2)[:, :, ::-1],
+                    scalar=r[:, h : h + 1],
+                    in1=tab_b[w][:, m - m0, :].rearrange("p (i e) -> p i e", e=2),
+                    op0=MULT,
+                    op1=MULT,
+                )
+                if (h + 1) % (4 // ADD_SPLIT) == 0:
+                    part = slice((h + 1 - 4 // ADD_SPLIT) * HD, (h + 1) * HD)
+                    nc.gpsimd.tensor_tensor(out=o[:, part], in0=t1[:, part], in1=t2[:, part], op=ADD)
+            nc.sync.dma_start(out=token_rows(dest[w])[:, m, c * CH : (c + 1) * CH], in_=o[:]) if m < 2 else nc.sync.dma_start(out=dest[w][256:1024, :].rearrange("(p j) n -> p j n", j=6)[:, m - 2, c * CH : (c + 1) * CH], in_=o[:])
+
+        banks = [(gi, m) for gi in range(4, len(groups)) for m in range(*tiles_of[groups[gi][0]])]
+        first = {}
+        for s, (gi, m) in enumerate(banks):
+            first.setdefault(gi, s)
+            first.setdefault(m // 2, s)
+        units = []
+        for gi, (kind, c) in enumerate(groups):
+            if kind == "x":
+                units.extend([(first[gi] - XLEAD, gi, g, 0) for g in range(PASSES)])
+            elif kind == "q":
+                order = [(g, half) for half in range(2) for g in range(PASSES)]
+                units.extend([(first[gi] - LEAD - (5 - i) * QSP, gi, g, half) for i, (g, half) in enumerate(order)])
+            else:
+                units.extend([(first[gi] - LEAD, gi, g, half) for g in range(PASSES) for half in range(2)])
+        units = sorted(units)
+        when = [0.0] * len(units)
+        t = 1000.0
+        for i in reversed(range(len(units))):
+            t = min(units[i][0], t - 1.0 / RMAX)
+            when[i] = t
+        left = {gi: sum(1 for u in units if u[1] == gi) for gi in range(len(groups))}
+        bf_groups = []
+        for u in units:
+            if groups[u[1]][0] in weight and u[1] not in bf_groups:
+                bf_groups.append(u[1])
+        q_groups = [gi for gi in range(len(groups)) if groups[gi][0] == "q"]
+
+        with tc.manual_schedule(engines=set(PIN)) if PIN else ExitStack():
+            nc.sync.dma_start(out=sq[:], in_=Wq_scale.rearrange("o (g p t) -> p (o g) t", p=P, t=4))
+            load_bytes(0)
+            nc.scalar.dma_start(out=g_bc[:, 0, :], in_=gain["q"].partition_broadcast(P))
+            for tab, src in ((cos_sb, rope_cos), (sin_sb, rope_sin)):
+                nc.scalar.dma_start(out=tab[:, 2:8, :], in_=src[256:1024, :].rearrange("(p j) d -> p j d", j=6))
+                nc.scalar.dma_start(out=tab[:, 0:2, :], in_=token_rows(src))
+            nc.scalar.activation(out=warm[:], in_=warm[:], func=(ACT.Abs_reciprocal_sqrt if RSQRT else ACT.Sqrt))
+            for gi in (1, 2, 3):
+                load_group(gi)
+            load_bytes(1)
+            load_group(bf_groups.pop(0))
+            for i, w in enumerate(names[1:]):
+                nc.sync.dma_start(out=g_bc[:, i + 1, :], in_=gain[w].partition_broadcast(P))
+            load_group(0)
+            for i in range(RAW_BUFS - 1):
+                load_group(bf_groups.pop(0))
+            load_bytes(2)
+            with nc.allow_non_contiguous_dma(reason="a bias value for each partition"):
+                for w in ("aq", "ak"):
+                    nc.sync.dma_start(out=b_col[w][:], in_=bias[w].rearrange("(h p) -> p h", p=P))
+            load_group(q_groups.pop(0))
+            cast(False)
+            cast(True)
+            cast(False)
+            cast(True)
+
+            g_pairs = g_bc[:].rearrange("p w (i e) -> p w i e", e=2)
+            gsw_pairs = gsw[:].rearrange("p w (i e) -> p w i e", e=2)
+            for i, w in enumerate(names):
+                m0, m1 = tiles_of[w]
+                nc.gpsimd.tensor_scalar(out=gsw_pairs[:, i, :, 0], in0=g_pairs[:, i, :, 1], scalar1=-1.0, scalar2=0.0, op0=MULT, op1=ADD)
+                nc.gpsimd.tensor_scalar(out=gsw_pairs[:, i, :, 1], in0=g_pairs[:, i, :, 0], scalar1=1.0, scalar2=0.0, op0=MULT, op1=ADD)
+                nc.gpsimd.tensor_tensor(out=tab_a[w][:], in0=cos_sb[:, m0:m1, :], in1=g_bc[:, i : i + 1, :].to_broadcast([P, m1 - m0, HD]), op=MULT)
+                nc.gpsimd.tensor_tensor(out=tab_b[w][:], in0=sin_sb[:, m0:m1, :], in1=gsw[:, i : i + 1, :].to_broadcast([P, m1 - m0, HD]), op=MULT)
+
+            state = {"units": 0}
+            products = []
+            quants = []
+            quanted = set()
+
+            def finish(gi, slot):
+                left[gi] -= 1
+                if left[gi] == 0:
+                    quants.append((gi, slot))
+
+            def advance(slot, upto_group):
+                while state["units"] < len(units) and (when[state["units"]] <= slot or any(left[gi] > 0 and u[1] == gi for gi in upto_group for u in units[state["units"] :])):
+                    gi, g, half = units[state["units"]][1:]
+                    kind = groups[gi][0]
+                    while casts and casts[0][0] == gi and casts[0][1] <= 2 * half + 1:
+                        cast(False)
+                    product = unit(gi, g, half)
+                    state["units"] += 1
+                    if product is None:
+                        finish(gi, slot)
+                    else:
+                        products.append((product, gi))
+                    if all(u[1] != gi for u in units[state["units"] :]):
+                        if kind in weight and bf_groups:
+                            load_group(bf_groups.pop(0))
+                        if kind == "q" and q_groups:
+                            load_group(q_groups.pop(0))
+
+            def product_now(slot):
+                product, gi = products.pop(0)
+                product()
+                finish(gi, slot - QLAG)
+
+            def quant_group(gi):
+                for g in range(PASSES):
+                    quant(gi, g)
+                quanted.add(gi)
+
+            def both_port_work(slot):
+                if products:
+                    product_now(slot)
+                while quants and quants[0][1] + QLAG <= slot:
+                    quant_group(quants.pop(0)[0])
+
+            for s in range(len(banks) + DELAY):
+                if s < len(banks):
+                    gi, m = banks[s]
+                    advance(s + PERIOD - 1 - s % PERIOD, (gi, m // 2))
+                    while any(p[1] == gi for p in products):
+                        product_now(s)
+                    while gi not in quanted or m // 2 not in quanted:
+                        quant_group(quants.pop(0)[0])
+                    if casts and s % 2 == 0:
+                        cast(False)
+                    if groups[gi][0] in bias and m == 0:
+                        text_heads(gi)
+                    bank_a(gi, m)
+                if s >= DELAY:
+                    bank_b(*banks[s - DELAY], lambda: both_port_work(s))

@@ -32,7 +32,7 @@ XLEAD = 1.0
 RMAX = 2.0
 QSP = 3.0
 PIN = (ENG.PE,)
-PERIOD = 2
+PERIOD = 1
 DUMMY = False
 CHUNKS = (("q", 0), ("k", 0), ("aq", 0), ("k", 1), ("ak", 0), ("q", 1), ("aq", 1), ("k", 2), ("ak", 1), ("aq", 2), ("ak", 2), ("q", 2))
 

@@ -76,8 +76,7 @@ def tile_flux2attention_pa_kernel(
         g_bc = const.tile([P, 4, HD], BF16, name="g_bc")
         gsw = const.tile([P, 4, HD], BF16, name="gsw")
         b_col = {w: const.tile([P, 12], BF16, name="b_col_" + w) for w in ("aq", "ak")}
-        tab_a = {w: const.tile([P, tiles_of[w][1] - tiles_of[w][0], HD], F32, name="tab_a_" + w) for w in names}
-        tab_b = {w: const.tile([P, tiles_of[w][1] - tiles_of[w][0], HD], F32, name="tab_b_" + w) for w in names}
+        rot = {w: const.tile([P, tiles_of[w][1] - tiles_of[w][0], 2, HD], F32, name="rot_" + w) for w in names}
         xc = const.tile([P, PASSES, 1024], U32, name="xc", align_bytes=64)
         xs = const.tile([P, PASSES, 1024], U8, name="xs", align_bytes=64)
 
@@ -226,25 +225,26 @@ def tile_flux2attention_pa_kernel(
             w, c = groups[gi]
             m0 = tiles_of[w][0]
             x, r = live.pop((gi, m))
-            t1 = epi.tile([P, CH], F32, name="t1")
-            t2 = epi.tile([P, CH], F32, name="t2")
+            t12 = epi.tile([P, 4, 2, HD], F32, name="t12")
             o = epi.tile([P, CH], F32, name="o")
             for h in range(4):
                 cols = slice(h * HD, (h + 1) * HD)
-                nc.vector.scalar_tensor_tensor(out=t1[:, cols], in0=x[:, cols], scalar=r[:, h : h + 1], in1=tab_a[w][:, m - m0, :], op0=MULT, op1=MULT)
                 if h == 3:
                     before_last()
                 nc.vector.scalar_tensor_tensor(
-                    out=t2[:, cols].rearrange("p (i e) -> p i e", e=2),
-                    in0=x[:, cols].rearrange("p (i e) -> p i e", e=2)[:, :, ::-1],
+                    out=t12[:, h, :, :],
+                    in0=x[:, cols].rearrange("p (o c) -> p o c", o=1).to_broadcast([P, 2, HD]),
                     scalar=r[:, h : h + 1],
-                    in1=tab_b[w][:, m - m0, :].rearrange("p (i e) -> p i e", e=2),
+                    in1=rot[w][:, m - m0, :, :],
                     op0=MULT,
                     op1=MULT,
                 )
-                if (h + 1) % (4 // ADD_SPLIT) == 0:
-                    part = slice((h + 1 - 4 // ADD_SPLIT) * HD, (h + 1) * HD)
-                    nc.gpsimd.tensor_tensor(out=o[:, part], in0=t1[:, part], in1=t2[:, part], op=ADD)
+            nc.gpsimd.tensor_tensor(
+                out=o[:].rearrange("p (h i e) -> p h i e", h=4, e=2),
+                in0=t12[:, :, 0, :].rearrange("p h (i e) -> p h i e", e=2),
+                in1=t12[:, :, 1, :].rearrange("p h (i e) -> p h i e", e=2)[:, :, :, ::-1],
+                op=ADD,
+            )
             nc.sync.dma_start(out=token_rows(dest[w])[:, m, c * CH : (c + 1) * CH], in_=o[:]) if m < 2 else nc.sync.dma_start(out=dest[w][256:1024, :].rearrange("(p j) n -> p j n", j=6)[:, m - 2, c * CH : (c + 1) * CH], in_=o[:])
 
         banks = [(gi, m) for gi in range(4, len(groups)) for m in range(*tiles_of[groups[gi][0]])]
@@ -305,10 +305,15 @@ def tile_flux2attention_pa_kernel(
             gsw_pairs = gsw[:].rearrange("p w (i e) -> p w i e", e=2)
             for i, w in enumerate(names):
                 m0, m1 = tiles_of[w]
-                nc.gpsimd.tensor_scalar(out=gsw_pairs[:, i, :, 0], in0=g_pairs[:, i, :, 1], scalar1=-1.0, scalar2=0.0, op0=MULT, op1=ADD)
-                nc.gpsimd.tensor_scalar(out=gsw_pairs[:, i, :, 1], in0=g_pairs[:, i, :, 0], scalar1=1.0, scalar2=0.0, op0=MULT, op1=ADD)
-                nc.gpsimd.tensor_tensor(out=tab_a[w][:], in0=cos_sb[:, m0:m1, :], in1=g_bc[:, i : i + 1, :].to_broadcast([P, m1 - m0, HD]), op=MULT)
-                nc.gpsimd.tensor_tensor(out=tab_b[w][:], in0=sin_sb[:, m0:m1, :], in1=gsw[:, i : i + 1, :].to_broadcast([P, m1 - m0, HD]), op=MULT)
+                nc.gpsimd.tensor_scalar(out=gsw_pairs[:, i, :, 0], in0=g_pairs[:, i, :, 0], scalar1=1.0, scalar2=0.0, op0=MULT, op1=ADD)
+                nc.gpsimd.tensor_scalar(out=gsw_pairs[:, i, :, 1], in0=g_pairs[:, i, :, 1], scalar1=-1.0, scalar2=0.0, op0=MULT, op1=ADD)
+                nc.gpsimd.tensor_tensor(out=rot[w][:, :, 0, :], in0=cos_sb[:, m0:m1, :], in1=g_bc[:, i : i + 1, :].to_broadcast([P, m1 - m0, HD]), op=MULT)
+                nc.gpsimd.tensor_tensor(
+                    out=rot[w][:, :, 1, :].rearrange("p m (i e) -> p m i e", e=2),
+                    in0=sin_sb[:, m0:m1, :].rearrange("p m (i e) -> p m i e", e=2)[:, :, :, ::-1],
+                    in1=gsw[:, i : i + 1, :].rearrange("p o (i e) -> p o i e", e=2).to_broadcast([P, m1 - m0, HD // 2, 2]),
+                    op=MULT,
+                )
 
             state = {"units": 0}
             products = []

@@ -28,12 +28,13 @@ DELAY = 2
 QLAG = 1
 ADD_SPLIT = 1
 LEAD = 3.0
-XLEAD = 1.0
+XLEAD = 3.0
 RMAX = 2.0
 QSP = 3.0
 PIN = (ENG.PE,)
 PERIOD = 1
 DUMMY = False
+LAST_ON_VECTOR = 2
 CHUNKS = (("q", 0), ("k", 0), ("aq", 0), ("k", 1), ("ak", 0), ("q", 1), ("aq", 1), ("k", 2), ("ak", 1), ("aq", 2), ("ak", 2), ("q", 2))
 
 
@@ -80,8 +81,6 @@ def tile_flux2attention_pa_kernel(
         xc = const.tile([P, PASSES, 1024], U32, name="xc", align_bytes=64)
         xs = const.tile([P, PASSES, 1024], U8, name="xs", align_bytes=64)
 
-        zeros = const.tile([P, CH], BF16, name="zeros")
-        nc.gpsimd.memset(zeros[:], 0.0)
         count = {"units": 0}
         raw_of = {}
         codes_of = {}
@@ -98,7 +97,11 @@ def tile_flux2attention_pa_kernel(
 
         def load_bytes(c):
             for half in range(2):
-                nc.sync.dma_start(out=byt[c][:, 2 * half : 2 * half + 2, :], in_=rows(Wq_bytes, c * CH + 256 * half, 2))
+                if c == 0 and half == 0:
+                    for g in range(PASSES):
+                        nc.sync.dma_start(out=byt[c][:, 0:2, g * CH : (g + 1) * CH], in_=rows(Wq_bytes, 0, 2)[:, :, g * CH : (g + 1) * CH])
+                else:
+                    nc.sync.dma_start(out=byt[c][:, 2 * half : 2 * half + 2, :], in_=rows(Wq_bytes, c * CH + 256 * half, 2))
 
         def load_group(gi):
             kind, c = groups[gi]
@@ -134,8 +137,6 @@ def tile_flux2attention_pa_kernel(
             gr = gr_of[(gi, g)]
             pt = ptp.tile([P, 2, 256], F32, name="pt")
             count["units"] += 1
-            if count["units"] % 3 != 0 and DUMMY:
-                nc.tensor.matmul(out=pt[:].rearrange("p u n -> p (u n)"), lhsT=zeros[:, 0:P], rhs=zeros[:], start=True, stop=True)
             for jj in range(2):
                 base = (2 * half + jj) * (D // 2) + 256 * g
                 for u in range(2):
@@ -239,7 +240,9 @@ def tile_flux2attention_pa_kernel(
                     op0=MULT,
                     op1=MULT,
                 )
-            nc.gpsimd.tensor_tensor(
+            count["panels"] = count.get("panels", 0) + 1
+            adder = nc.vector if count["panels"] > len(banks) - LAST_ON_VECTOR else nc.gpsimd
+            adder.tensor_tensor(
                 out=o[:].rearrange("p (h i e) -> p h i e", h=4, e=2),
                 in0=t12[:, :, 0, :].rearrange("p h (i e) -> p h i e", e=2),
                 in1=t12[:, :, 1, :].rearrange("p h (i e) -> p h i e", e=2)[:, :, :, ::-1],
@@ -296,10 +299,16 @@ def tile_flux2attention_pa_kernel(
                 for w in ("aq", "ak"):
                     nc.sync.dma_start(out=b_col[w][:], in_=bias[w].rearrange("(h p) -> p h", p=P))
             load_group(q_groups.pop(0))
-            cast(False)
-            cast(True)
-            cast(False)
-            cast(True)
+            first_q = casts[0][0]
+            casts.clear()
+
+            def first_casts(g, half):
+                cols = slice(g * CH, (g + 1) * CH)
+                for j in (2 * half, 2 * half + 1):
+                    if half == 0:
+                        nc.vector.tensor_copy(out=raw_of[first_q][:, j, cols], in_=byt[0][:, j, cols].bitcast(FP8))
+                    else:
+                        nc.scalar.copy(out=raw_of[first_q][:, j, cols], in_=byt[0][:, j, cols].bitcast(FP8))
 
             g_pairs = g_bc[:].rearrange("p w (i e) -> p w i e", e=2)
             gsw_pairs = gsw[:].rearrange("p w (i e) -> p w i e", e=2)
@@ -331,6 +340,8 @@ def tile_flux2attention_pa_kernel(
                     kind = groups[gi][0]
                     while casts and casts[0][0] == gi and casts[0][1] <= 2 * half + 1:
                         cast(False)
+                    if gi == first_q:
+                        first_casts(g, half)
                     product = unit(gi, g, half)
                     state["units"] += 1
                     if product is None:
@@ -362,6 +373,9 @@ def tile_flux2attention_pa_kernel(
             for s in range(len(banks) + DELAY):
                 if s < len(banks):
                     gi, m = banks[s]
+                    early = groups[gi][0] in bias and m == 0 and gi in quanted and 0 in quanted
+                    if early:
+                        text_heads(gi)
                     advance(s + PERIOD - 1 - s % PERIOD, (gi, m // 2))
                     while any(p[1] == gi for p in products):
                         product_now(s)
@@ -369,7 +383,7 @@ def tile_flux2attention_pa_kernel(
                         quant_group(quants.pop(0)[0])
                     if casts and s % 2 == 0:
                         cast(False)
-                    if groups[gi][0] in bias and m == 0:
+                    if groups[gi][0] in bias and m == 0 and not early:
                         text_heads(gi)
                     bank_a(gi, m)
                 if s >= DELAY:

@@ -31,7 +31,8 @@ LEAD = 3.0
 XLEAD = 3.0
 RMAX = 2.0
 QSP = 3.0
-PIN = (ENG.PE,)
+PIN = (ENG.PE, ENG.Pool)
+TAB_LEAD = 6
 PERIOD = 1
 DUMMY = False
 LAST_ON_VECTOR = 2
@@ -312,17 +313,36 @@ def tile_flux2attention_pa_kernel(
 
             g_pairs = g_bc[:].rearrange("p w (i e) -> p w i e", e=2)
             gsw_pairs = gsw[:].rearrange("p w (i e) -> p w i e", e=2)
-            for i, w in enumerate(names):
-                m0, m1 = tiles_of[w]
+            tables = []
+
+            def signed_gain(i):
                 nc.gpsimd.tensor_scalar(out=gsw_pairs[:, i, :, 0], in0=g_pairs[:, i, :, 0], scalar1=1.0, scalar2=0.0, op0=MULT, op1=ADD)
                 nc.gpsimd.tensor_scalar(out=gsw_pairs[:, i, :, 1], in0=g_pairs[:, i, :, 1], scalar1=-1.0, scalar2=0.0, op0=MULT, op1=ADD)
-                nc.gpsimd.tensor_tensor(out=rot[w][:, :, 0, :], in0=cos_sb[:, m0:m1, :], in1=g_bc[:, i : i + 1, :].to_broadcast([P, m1 - m0, HD]), op=MULT)
+
+            def table(i, m):
+                w = names[i]
+                j = m - tiles_of[w][0]
+                nc.gpsimd.tensor_tensor(out=rot[w][:, j, 0, :], in0=cos_sb[:, m, :], in1=g_bc[:, i, :], op=MULT)
                 nc.gpsimd.tensor_tensor(
-                    out=rot[w][:, :, 1, :].rearrange("p m (i e) -> p m i e", e=2),
-                    in0=sin_sb[:, m0:m1, :].rearrange("p m (i e) -> p m i e", e=2)[:, :, :, ::-1],
-                    in1=gsw[:, i : i + 1, :].rearrange("p o (i e) -> p o i e", e=2).to_broadcast([P, m1 - m0, HD // 2, 2]),
+                    out=rot[w][:, j, 1, :].rearrange("p (i e) -> p i e", e=2),
+                    in0=sin_sb[:, m, :].rearrange("p (i e) -> p i e", e=2)[:, :, ::-1],
+                    in1=gsw[:, i, :].rearrange("p (i e) -> p i e", e=2),
                     op=MULT,
                 )
+
+            for i, w in enumerate(names):
+                start = min(s for s, (gi, m) in enumerate(banks) if groups[gi][0] == w)
+                tables.extend([(start - TAB_LEAD + m - tiles_of[w][0], i, m) for m in range(*tiles_of[w])])
+            tables = sorted(tables)
+
+            def tables_upto(slot):
+                while tables and tables[0][0] <= slot:
+                    i, m = tables.pop(0)[1:]
+                    if m == tiles_of[names[i]][0]:
+                        signed_gain(i)
+                    table(i, m)
+
+            tables_upto(-1)
 
             state = {"units": 0}
             products = []
@@ -388,3 +408,4 @@ def tile_flux2attention_pa_kernel(
                     bank_a(gi, m)
                 if s >= DELAY:
                     bank_b(*banks[s - DELAY], lambda: both_port_work(s))
+                tables_upto(s)

@@ -23,18 +23,14 @@ EPS = 1e-5
 FLOPS = 2 * 1024 * 1536 * 3072
 
 RAW_BUFS = 3
-RSQRT = True
 DELAY = 2
 QLAG = 1
-ADD_SPLIT = 1
 LEAD = 3.0
 XLEAD = 3.0
 RMAX = 2.0
 QSP = 3.0
 PIN = (ENG.PE, ENG.Pool)
-TAB_LEAD = 6
 PERIOD = 1
-DUMMY = False
 LAST_ON_VECTOR = 2
 CHUNKS = (("q", 0), ("k", 0), ("aq", 0), ("k", 1), ("ak", 0), ("q", 1), ("aq", 1), ("k", 2), ("ak", 1), ("aq", 2), ("ak", 2), ("q", 2))
 
@@ -69,6 +65,8 @@ def tile_flux2attention_pa_kernel(
         ident = const.tile([P, P], F32, name="ident")
         make_identity(nc, ident[:])
         warm = const.tile([P, 1], F32, name="warm")
+        gate = const.tile([P, 2], BF16, name="gate")
+        gate2 = const.tile([P, 2], F32, name="gate2")
         nc.vector.memset(warm[:], 1.0)
 
         sq = const.tile([P, PASSES, 4], F32, name="sq")
@@ -215,12 +213,7 @@ def tile_flux2attention_pa_kernel(
             for h in range(4):
                 junk = epi.tile([P, HD], BF16, name="junk")
                 nc.scalar.activation(out=junk[:], in_=ps[:, h * HD : (h + 1) * HD], func=ACT.Square, accum_out=ss[:, h : h + 1])
-            if RSQRT:
-                nc.scalar.activation(out=r[:], in_=ss[:], func=ACT.Abs_reciprocal_sqrt, scale=1.0 / HD, bias=EPS)
-            else:
-                rt = stat.tile([P, 4], F32, name="rt")
-                nc.scalar.activation(out=rt[:], in_=ss[:], func=ACT.Sqrt, scale=1.0 / HD, bias=EPS)
-                nc.vector.reciprocal(out=r[:], in_=rt[:])
+            nc.scalar.activation(out=r[:], in_=ss[:], func=ACT.Abs_reciprocal_sqrt, scale=1.0 / HD, bias=EPS)
             live[(gi, m)] = (ps, r)
 
         def bank_b(gi, m, before_last):
@@ -281,17 +274,18 @@ def tile_flux2attention_pa_kernel(
         with tc.manual_schedule(engines=set(PIN)) if PIN else ExitStack():
             nc.sync.dma_start(out=sq[:], in_=Wq_scale.rearrange("o (g p t) -> p (o g) t", p=P, t=4))
             load_bytes(0)
-            nc.scalar.dma_start(out=g_bc[:, 0, :], in_=gain["q"].partition_broadcast(P))
+            for i in range(2):
+                nc.scalar.dma_start(out=g_bc[:, i, :], in_=gain[names[i]].partition_broadcast(P))
             for tab, src in ((cos_sb, rope_cos), (sin_sb, rope_sin)):
                 nc.scalar.dma_start(out=tab[:, 2:8, :], in_=src[256:1024, :].rearrange("(p j) d -> p j d", j=6))
                 nc.scalar.dma_start(out=tab[:, 0:2, :], in_=token_rows(src))
-            nc.scalar.activation(out=warm[:], in_=warm[:], func=(ACT.Abs_reciprocal_sqrt if RSQRT else ACT.Sqrt))
+            nc.scalar.activation(out=warm[:], in_=warm[:], func=ACT.Abs_reciprocal_sqrt)
             for gi in (1, 2, 3):
                 load_group(gi)
             load_bytes(1)
             load_group(bf_groups.pop(0))
-            for i, w in enumerate(names[1:]):
-                nc.sync.dma_start(out=g_bc[:, i + 1, :], in_=gain[w].partition_broadcast(P))
+            for i in (2, 3):
+                nc.sync.dma_start(out=g_bc[:, i, :], in_=gain[names[i]].partition_broadcast(P))
             load_group(0)
             for i in range(RAW_BUFS - 1):
                 load_group(bf_groups.pop(0))
@@ -313,36 +307,38 @@ def tile_flux2attention_pa_kernel(
 
             g_pairs = g_bc[:].rearrange("p w (i e) -> p w i e", e=2)
             gsw_pairs = gsw[:].rearrange("p w (i e) -> p w i e", e=2)
-            tables = []
 
             def signed_gain(i):
                 nc.gpsimd.tensor_scalar(out=gsw_pairs[:, i, :, 0], in0=g_pairs[:, i, :, 0], scalar1=1.0, scalar2=0.0, op0=MULT, op1=ADD)
                 nc.gpsimd.tensor_scalar(out=gsw_pairs[:, i, :, 1], in0=g_pairs[:, i, :, 1], scalar1=-1.0, scalar2=0.0, op0=MULT, op1=ADD)
 
-            def table(i, m):
+            def tables_of(i):
                 w = names[i]
-                j = m - tiles_of[w][0]
-                nc.gpsimd.tensor_tensor(out=rot[w][:, j, 0, :], in0=cos_sb[:, m, :], in1=g_bc[:, i, :], op=MULT)
+                lo, hi = tiles_of[w]
+                n = hi - lo
+                signed_gain(i)
                 nc.gpsimd.tensor_tensor(
-                    out=rot[w][:, j, 1, :].rearrange("p (i e) -> p i e", e=2),
-                    in0=sin_sb[:, m, :].rearrange("p (i e) -> p i e", e=2)[:, :, ::-1],
-                    in1=gsw[:, i, :].rearrange("p (i e) -> p i e", e=2),
+                    out=rot[w][:, :, 0, :],
+                    in0=cos_sb[:, lo:hi, :],
+                    in1=g_bc[:, i, :].rearrange("p (o d) -> p o d", o=1).to_broadcast([P, n, HD]),
+                    op=MULT,
+                )
+                nc.gpsimd.tensor_tensor(
+                    out=rot[w][:, :, 1, :].rearrange("p j (i e) -> p j i e", e=2),
+                    in0=sin_sb[:, lo:hi, :].rearrange("p j (i e) -> p j i e", e=2)[:, :, :, ::-1],
+                    in1=gsw[:, i, :].rearrange("p (o i e) -> p o i e", o=1, e=2).to_broadcast([P, n, HD // 2, 2]),
                     op=MULT,
                 )
 
-            for i, w in enumerate(names):
-                start = min(s for s, (gi, m) in enumerate(banks) if groups[gi][0] == w)
-                tables.extend([(start - TAB_LEAD + m - tiles_of[w][0], i, m) for m in range(*tiles_of[w])])
-            tables = sorted(tables)
+            def first_tables():
+                nc.gpsimd.tensor_copy(out=gate[:], in_=raw_of[first_q][:, 1, D - 2 : D])
+                tables_of(0)
+                tables_of(1)
 
-            def tables_upto(slot):
-                while tables and tables[0][0] <= slot:
-                    i, m = tables.pop(0)[1:]
-                    if m == tiles_of[names[i]][0]:
-                        signed_gain(i)
-                    table(i, m)
-
-            tables_upto(-1)
+            def text_tables():
+                nc.gpsimd.tensor_copy(out=gate2[:], in_=live[banks[0]][1][:, 0:2])
+                tables_of(2)
+                tables_of(3)
 
             state = {"units": 0}
             products = []
@@ -362,6 +358,8 @@ def tile_flux2attention_pa_kernel(
                         cast(False)
                     if gi == first_q:
                         first_casts(g, half)
+                        if (g, half) == (PASSES - 1, 0):
+                            first_tables()
                     product = unit(gi, g, half)
                     state["units"] += 1
                     if product is None:
@@ -406,6 +404,7 @@ def tile_flux2attention_pa_kernel(
                     if groups[gi][0] in bias and m == 0 and not early:
                         text_heads(gi)
                     bank_a(gi, m)
+                    if s == 0:
+                        text_tables()
                 if s >= DELAY:
                     bank_b(*banks[s - DELAY], lambda: both_port_work(s))
-                tables_upto(s)

@@ -64,6 +64,8 @@ def tile_flux2attention_pa_kernel(
 
         ident = const.tile([P, P], F32, name="ident")
         make_identity(nc, ident[:])
+        ident_bf = const.tile([P, P], BF16, name="ident_bf")
+        make_identity(nc, ident_bf[:])
         warm = const.tile([P, 1], F32, name="warm")
         gate = const.tile([P, 2], BF16, name="gate")
         gate2 = const.tile([P, 2], F32, name="gate2")
@@ -80,7 +82,7 @@ def tile_flux2attention_pa_kernel(
         xc = const.tile([P, PASSES, 1024], U32, name="xc", align_bytes=64)
         xs = const.tile([P, PASSES, 1024], U8, name="xs", align_bytes=64)
 
-        count = {"units": 0}
+        count = {}
         raw_of = {}
         codes_of = {}
         gr_of = {}
@@ -134,22 +136,30 @@ def tile_flux2attention_pa_kernel(
                 else:
                     gr_of[(gi, g)] = grp.tile([P, CH * 4], BF16, name="gr", align_bytes=64)
             gr = gr_of[(gi, g)]
+            if kind == "q":
+                pq = ptp.tile([P, 4, 256], BF16, name="pt")
+                for jj in range(2):
+                    for t in range(4):
+                        nc.tensor.matmul(
+                            pq[:, t, jj * P : (jj + 1) * P],
+                            lhsT=raw_of[gi][:, 2 * half + jj, CH * g + t : CH * (g + 1) : 4],
+                            rhs=ident_bf[:],
+                            start=True,
+                            stop=True,
+                        )
+                return lambda: nc.vector.tensor_tensor(
+                    out=gr[:, half * 1024 : (half + 1) * 1024].rearrange("p (n t) -> p n t", t=4),
+                    in0=pq[:].rearrange("p t n -> p n t"),
+                    in1=sq[:, g, :].rearrange("p (o t) -> p o t", o=1).to_broadcast([P, 256, 4]),
+                    op=MULT,
+                )
             pt = ptp.tile([P, 2, 256], F32, name="pt")
-            count["units"] += 1
             for jj in range(2):
                 base = (2 * half + jj) * (D // 2) + 256 * g
                 for u in range(2):
                     nc.tensor.transpose(pt[:, u, jj * P : (jj + 1) * P], words[:, base + u : base + 256 : 2], ident[:])
-            if kind == "q":
-                return lambda: nc.vector.tensor_tensor(
-                    out=gr[:, half * 1024 : (half + 1) * 1024].rearrange("p (n u e) -> p n u e", u=2, e=2),
-                    in0=pt[:].rearrange("p u n -> p (u n)").bitcast(BF16).rearrange("p (u n e) -> p n u e", u=2, e=2),
-                    in1=sq[:, g, :].rearrange("p (o u e) -> p o u e", o=1, u=2).to_broadcast([P, 256, 2, 2]),
-                    op=MULT,
-                )
-            else:
-                gr_words = gr[:].bitcast(F32).rearrange("p (n u) -> p n u", u=2)
-                nc.scalar.copy(out=gr_words[:, half * 256 : (half + 1) * 256, :], in_=pt[:].rearrange("p u n -> p n u"))
+            gr_words = gr[:].bitcast(F32).rearrange("p (n u) -> p n u", u=2)
+            nc.scalar.copy(out=gr_words[:, half * 256 : (half + 1) * 256, :], in_=pt[:].rearrange("p u n -> p n u"))
             return None
 
         def quant(gi, g):
@@ -272,20 +282,22 @@ def tile_flux2attention_pa_kernel(
         q_groups = [gi for gi in range(len(groups)) if groups[gi][0] == "q"]
 
         with tc.manual_schedule(engines=set(PIN)) if PIN else ExitStack():
-            nc.sync.dma_start(out=sq[:], in_=Wq_scale.rearrange("o (g p t) -> p (o g) t", p=P, t=4))
-            load_bytes(0)
-            for i in range(2):
-                nc.scalar.dma_start(out=g_bc[:, i, :], in_=gain[names[i]].partition_broadcast(P))
-            for tab, src in ((cos_sb, rope_cos), (sin_sb, rope_sin)):
-                nc.scalar.dma_start(out=tab[:, 2:8, :], in_=src[256:1024, :].rearrange("(p j) d -> p j d", j=6))
-                nc.scalar.dma_start(out=tab[:, 0:2, :], in_=token_rows(src))
             nc.scalar.activation(out=warm[:], in_=warm[:], func=ACT.Abs_reciprocal_sqrt)
-            for gi in (1, 2, 3):
-                load_group(gi)
+            load_bytes(0)
+            nc.sync.dma_start(out=sq[:], in_=Wq_scale.rearrange("o (g p t) -> p (o g) t", p=P, t=4))
+            load_group(1)
+            for i in range(2):
+                nc.sync.dma_start(out=g_bc[:, i, :], in_=gain[names[i]].partition_broadcast(P))
+            for tab, src in ((cos_sb, rope_cos), (sin_sb, rope_sin)):
+                nc.sync.dma_start(out=tab[:, 2:8, :], in_=src[256:1024, :].rearrange("(p j) d -> p j d", j=6))
+            load_group(2)
+            load_group(3)
             load_bytes(1)
             load_group(bf_groups.pop(0))
             for i in (2, 3):
                 nc.sync.dma_start(out=g_bc[:, i, :], in_=gain[names[i]].partition_broadcast(P))
+            for tab, src in ((cos_sb, rope_cos), (sin_sb, rope_sin)):
+                nc.sync.dma_start(out=tab[:, 0:2, :], in_=token_rows(src))
             load_group(0)
             for i in range(RAW_BUFS - 1):
                 load_group(bf_groups.pop(0))

from contextlib import ExitStack

import concourse.mybir as mybir
from concourse.masks import make_identity

F32 = mybir.dt.float32
BF16 = mybir.dt.bfloat16
U32 = mybir.dt.uint32
U8 = mybir.dt.uint8
FP8 = mybir.dt.float8_e4m3fn
FP8X4 = mybir.dt.float8_e4m3fn_x4
MULT = mybir.AluOpType.mult
ADD = mybir.AluOpType.add
ACT = mybir.ActivationFunctionType
ENG = mybir.EngineType

P = 128
D = 1536
HD = 128
PASSES = 3
CH = 512
EPS = 1e-5
FLOPS = 2 * 1024 * 1536 * 3072

RAW_BUFS = 3
DELAY = 2
QLAG = 1
LEAD = 3.0
XLEAD = 3.0
RMAX = 2.0
QSP = 3.0
PIN = (ENG.PE, ENG.Pool)
PERIOD = 1
LAST_ON_VECTOR = 2
CHUNKS = (("q", 0), ("k", 0), ("aq", 0), ("k", 1), ("ak", 0), ("q", 1), ("aq", 1), ("k", 2), ("ak", 1), ("aq", 2), ("ak", 2), ("q", 2))


def tile_flux2attention_pa_kernel(
    tc, hidden_states, encoder_hidden_states, rope_cos, rope_sin, Wq_bytes, Wq_scale, Wk, Waq, baq, Wak, bak,
    wq_norm, wk_norm, waq_norm, wak_norm, out_0, out_1,
):
    nc = tc.nc
    hid = hidden_states.flatten_outer_dims()
    enc = encoder_hidden_states.flatten_outer_dims()
    out_q = out_0.rearrange("b s h d -> (b s) (h d)")
    out_k = out_1.rearrange("b s h d -> (b s) (h d)")
    dest = {"q": out_q, "aq": out_q, "k": out_k, "ak": out_k}
    weight = {"k": Wk, "aq": Waq, "ak": Wak}
    gain = {"q": wq_norm, "k": wk_norm, "aq": waq_norm, "ak": wak_norm}
    bias = {"aq": baq, "ak": bak}
    tiles_of = {"q": (2, 8), "k": (2, 8), "aq": (0, 2), "ak": (0, 2)}
    names = ("q", "k", "aq", "ak")
    groups = [("x", i) for i in range(4)] + list(CHUNKS)

    with ExitStack() as ctx:
        const = ctx.enter_context(tc.tile_pool(name="const", bufs=1))
        rawp = ctx.enter_context(tc.tile_pool(name="rawp", bufs=RAW_BUFS))
        grp = ctx.enter_context(tc.tile_pool(name="grp", bufs=4))
        wcp = ctx.enter_context(tc.tile_pool(name="wcp", bufs=4))
        epi = ctx.enter_context(tc.tile_pool(name="epi", bufs=4))
        stat = ctx.enter_context(tc.tile_pool(name="stat", bufs=8))
        ptp = ctx.enter_context(tc.psum_pool(name="ptp", bufs=4))
        pmp = ctx.enter_context(tc.psum_pool(name="pmp", bufs=4))

        ident = const.tile([P, P], F32, name="ident")
        make_identity(nc, ident[:])
        ident_bf = const.tile([P, P], BF16, name="ident_bf")
        make_identity(nc, ident_bf[:])
        warm = const.tile([P, 1], F32, name="warm")
        gate = const.tile([P, 2], BF16, name="gate")
        gate2 = const.tile([P, 2], F32, name="gate2")
        nc.vector.memset(warm[:], 1.0)

        sq = const.tile([P, PASSES, 4], F32, name="sq")
        byt = [const.tile([P, 4, D], U8, name="byt%d" % c) for c in range(3)]
        cos_sb = const.tile([P, 8, HD], BF16, name="cos_sb")
        sin_sb = const.tile([P, 8, HD], BF16, name="sin_sb")
        g_bc = const.tile([P, 4, HD], BF16, name="g_bc")
        gsw = const.tile([P, 4, HD], BF16, name="gsw")
        b_col = {w: const.tile([P, 12], BF16, name="b_col_" + w) for w in ("aq", "ak")}
        rot = {w: const.tile([P, tiles_of[w][1] - tiles_of[w][0], 2, HD], F32, name="rot_" + w) for w in names}
        xc = const.tile([P, PASSES, 1024], U32, name="xc", align_bytes=64)
        xs = const.tile([P, PASSES, 1024], U8, name="xs", align_bytes=64)

        count = {}
        raw_of = {}
        codes_of = {}
        gr_of = {}
        xbt_of = {}
        casts = []
        live = {}

        def token_rows(src):
            return src[0:256, :].rearrange("(p j) n -> p j n", j=2)

        def rows(src, r0, n):
            return src[r0 : r0 + n * P, :].rearrange("(j p) k -> p j k", p=P)

        def load_bytes(c):
            for half in range(2):
                if c == 0 and half == 0:
                    for g in range(PASSES):
                        nc.sync.dma_start(out=byt[c][:, 0:2, g * CH : (g + 1) * CH], in_=rows(Wq_bytes, 0, 2)[:, :, g * CH : (g + 1) * CH])
                else:
                    nc.sync.dma_start(out=byt[c][:, 2 * half : 2 * half + 2, :], in_=rows(Wq_bytes, c * CH + 256 * half, 2))

        def load_group(gi):
            kind, c = groups[gi]
            if kind == "x":
                raw = rawp.tile([P, 2, D], BF16, name="rawx", bufs=4)
                nc.sync.dma_start(out=raw[:], in_=(enc.rearrange("(p j) k -> p j k", j=2) if c == 0 else hid.rearrange("(p j) k -> p j k", j=6)[:, 2 * c - 2 : 2 * c, :]))
            elif kind == "q":
                raw = rawp.tile([P, 4, D], BF16, name="rawq", bufs=1)
                casts.extend([(gi, j) for j in range(4)])
            else:
                raw = rawp.tile([P, 4, D], BF16, name="raw")
                nc.sync.dma_start(out=raw[:], in_=rows(weight[kind], c * CH, 4))
            raw_of[gi] = raw

        def cast(on_vector):
            gi, j = casts.pop(0)
            src = byt[groups[gi][1]][:, j, :].bitcast(FP8)
            if on_vector:
                nc.vector.tensor_copy(out=raw_of[gi][:, j, :], in_=src)
            else:
                nc.scalar.copy(out=raw_of[gi][:, j, :], in_=src)

        def unit(gi, g, half):
            kind, c = groups[gi]
            words = raw_of[gi][:].rearrange("p j k -> p (j k)").bitcast(F32)
            if (gi, g) not in gr_of:
                if kind == "x":
                    gr_of[(gi, g)] = grp.tile([P, 1024], BF16, name="grx", align_bytes=64)
                elif kind == "q":
                    gr_of[(gi, g)] = grp.tile([P, CH * 4], BF16, name="grq", align_bytes=64, bufs=3)
                else:
                    gr_of[(gi, g)] = grp.tile([P, CH * 4], BF16, name="gr", align_bytes=64)
            gr = gr_of[(gi, g)]
            if kind == "q":
                pq = ptp.tile([P, 4, 256], BF16, name="pt")
                for jj in range(2):
                    for t in range(4):
                        nc.tensor.matmul(
                            pq[:, t, jj * P : (jj + 1) * P],
                            lhsT=raw_of[gi][:, 2 * half + jj, CH * g + t : CH * (g + 1) : 4],
                            rhs=ident_bf[:],
                            start=True,
                            stop=True,
                        )
                return lambda: nc.vector.tensor_tensor(
                    out=gr[:, half * 1024 : (half + 1) * 1024].rearrange("p (n t) -> p n t", t=4),
                    in0=pq[:].rearrange("p t n -> p n t"),
                    in1=sq[:, g, :].rearrange("p (o t) -> p o t", o=1).to_broadcast([P, 256, 4]),
                    op=MULT,
                )
            pt = ptp.tile([P, 2, 256], F32, name="pt")
            for jj in range(2):
                base = (2 * half + jj) * (D // 2) + 256 * g
                for u in range(2):
                    nc.tensor.transpose(pt[:, u, jj * P : (jj + 1) * P], words[:, base + u : base + 256 : 2], ident[:])
            gr_words = gr[:].bitcast(F32).rearrange("p (n u) -> p n u", u=2)
            nc.scalar.copy(out=gr_words[:, half * 256 : (half + 1) * 256, :], in_=pt[:].rearrange("p u n -> p n u"))
            return None

        def quant(gi, g):
            kind, c = groups[gi]
            if kind == "x":
                codes = xc[:, g, c * 256 : (c + 1) * 256]
                scales = xs[:, g, c * 256 : (c + 1) * 256]
            else:
                if gi not in codes_of:
                    wc = wcp.tile([P, PASSES, CH], U32, name="wc", align_bytes=64)
                    ws = wcp.tile([P, PASSES, CH], U8, name="ws", align_bytes=64)
                    codes_of[gi] = (wc, ws)
                wc, ws = codes_of[gi]
                codes = wc[:, g, :]
                scales = ws[:, g, :]
            nc.vector.quantize_mx(out=codes.bitcast(FP8X4), scales=scales, in_=gr_of[(gi, g)][:])

        def text_heads(gi):
            w, c = groups[gi]
            wc, ws = codes_of[gi]
            xbt = epi.tile([P, 4, 256], F32, name="xbt", bufs=2)
            xbt_of[gi] = xbt
            for hp in range(2):
                pt = ptp.tile([P, 2, 256], F32, name="pt")
                for hh in range(2):
                    cols = slice((2 * hp + hh) * HD, (2 * hp + hh + 1) * HD)
                    for g in range(PASSES):
                        nc.tensor.matmul_mx(
                            out=pt[:, hh, :],
                            lhsT=wc[:, g, cols].bitcast(FP8X4),
                            lhsT_scale=ws[:, g, cols],
                            rhs=xc[:, g, 0:256].bitcast(FP8X4),
                            rhs_scale=xs[:, g, 0:256],
                            start=(g == 0),
                            stop=(g == PASSES - 1),
                        )
                for hh in range(2):
                    h = 2 * hp + hh
                    nc.scalar.activation(out=xbt[:, h, :], in_=pt[:, hh, :], func=ACT.Identity, bias=b_col[w][:, 4 * c + h : 4 * c + h + 1])

        def bank_a(gi, m):
            w, c = groups[gi]
            ps = pmp.tile([P, CH], F32, name="ps")
            if w in bias:
                for h in range(4):
                    nc.tensor.transpose(ps[:, h * HD : (h + 1) * HD], xbt_of[gi][:, h, m * P : (m + 1) * P], ident[:])
            else:
                wc, ws = codes_of[gi]
                for g in range(PASSES):
                    nc.tensor.matmul_mx(
                        out=ps[:],
                        lhsT=xc[:, g, m * P : (m + 1) * P].bitcast(FP8X4),
                        lhsT_scale=xs[:, g, m * P : (m + 1) * P],
                        rhs=wc[:, g, :].bitcast(FP8X4),
                        rhs_scale=ws[:, g, :],
                        start=(g == 0),
                        stop=(g == PASSES - 1),
                    )
            ss = stat.tile([P, 4], F32, name="ss")
            r = stat.tile([P, 4], F32, name="r")
            for h in range(4):
                junk = epi.tile([P, HD], BF16, name="junk")
                nc.scalar.activation(out=junk[:], in_=ps[:, h * HD : (h + 1) * HD], func=ACT.Square, accum_out=ss[:, h : h + 1])
            nc.scalar.activation(out=r[:], in_=ss[:], func=ACT.Abs_reciprocal_sqrt, scale=1.0 / HD, bias=EPS)
            live[(gi, m)] = (ps, r)

        def bank_b(gi, m, before_last):
            w, c = groups[gi]
            m0 = tiles_of[w][0]
            x, r = live.pop((gi, m))
            t12 = epi.tile([P, 4, 2, HD], F32, name="t12")
            o = epi.tile([P, CH], F32, name="o")
            for h in range(4):
                cols = slice(h * HD, (h + 1) * HD)
                if h == 3:
                    before_last()
                nc.vector.scalar_tensor_tensor(
                    out=t12[:, h, :, :],
                    in0=x[:, cols].rearrange("p (o c) -> p o c", o=1).to_broadcast([P, 2, HD]),
                    scalar=r[:, h : h + 1],
                    in1=rot[w][:, m - m0, :, :],
                    op0=MULT,
                    op1=MULT,
                )
            count["panels"] = count.get("panels", 0) + 1
            adder = nc.vector if count["panels"] > len(banks) - LAST_ON_VECTOR else nc.gpsimd
            adder.tensor_tensor(
                out=o[:].rearrange("p (h i e) -> p h i e", h=4, e=2),
                in0=t12[:, :, 0, :].rearrange("p h (i e) -> p h i e", e=2),
                in1=t12[:, :, 1, :].rearrange("p h (i e) -> p h i e", e=2)[:, :, :, ::-1],
                op=ADD,
            )
            nc.sync.dma_start(out=token_rows(dest[w])[:, m, c * CH : (c + 1) * CH], in_=o[:]) if m < 2 else nc.sync.dma_start(out=dest[w][256:1024, :].rearrange("(p j) n -> p j n", j=6)[:, m - 2, c * CH : (c + 1) * CH], in_=o[:])

        banks = [(gi, m) for gi in range(4, len(groups)) for m in range(*tiles_of[groups[gi][0]])]
        first = {}
        for s, (gi, m) in enumerate(banks):
            first.setdefault(gi, s)
            first.setdefault(m // 2, s)
        units = []
        for gi, (kind, c) in enumerate(groups):
            if kind == "x":
                units.extend([(first[gi] - XLEAD, gi, g, 0) for g in range(PASSES)])
            elif kind == "q":
                order = [(g, half) for half in range(2) for g in range(PASSES)]
                units.extend([(first[gi] - LEAD - (5 - i) * QSP, gi, g, half) for i, (g, half) in enumerate(order)])
            else:
                units.extend([(first[gi] - LEAD, gi, g, half) for g in range(PASSES) for half in range(2)])
        units = sorted(units)
        when = [0.0] * len(units)
        t = 1000.0
        for i in reversed(range(len(units))):
            t = min(units[i][0], t - 1.0 / RMAX)
            when[i] = t
        left = {gi: sum(1 for u in units if u[1] == gi) for gi in range(len(groups))}
        bf_groups = []
        for u in units:
            if groups[u[1]][0] in weight and u[1] not in bf_groups:
                bf_groups.append(u[1])
        q_groups = [gi for gi in range(len(groups)) if groups[gi][0] == "q"]

        with tc.manual_schedule(engines=set(PIN)) if PIN else ExitStack():
            nc.scalar.activation(out=warm[:], in_=warm[:], func=ACT.Abs_reciprocal_sqrt)
            load_bytes(0)
            nc.sync.dma_start(out=sq[:], in_=Wq_scale.rearrange("o (g p t) -> p (o g) t", p=P, t=4))
            load_group(1)
            for i in range(2):
                nc.sync.dma_start(out=g_bc[:, i, :], in_=gain[names[i]].partition_broadcast(P))
            for tab, src in ((cos_sb, rope_cos), (sin_sb, rope_sin)):
                nc.sync.dma_start(out=tab[:, 2:8, :], in_=src[256:1024, :].rearrange("(p j) d -> p j d", j=6))
            load_group(2)
            load_group(3)
            load_bytes(1)
            load_group(bf_groups.pop(0))
            for i in (2, 3):
                nc.sync.dma_start(out=g_bc[:, i, :], in_=gain[names[i]].partition_broadcast(P))
            for tab, src in ((cos_sb, rope_cos), (sin_sb, rope_sin)):
                nc.sync.dma_start(out=tab[:, 0:2, :], in_=token_rows(src))
            load_group(0)
            for i in range(RAW_BUFS - 1):
                load_group(bf_groups.pop(0))
            load_bytes(2)
            with nc.allow_non_contiguous_dma(reason="a bias value for each partition"):
                for w in ("aq", "ak"):
                    nc.sync.dma_start(out=b_col[w][:], in_=bias[w].rearrange("(h p) -> p h", p=P))
            load_group(q_groups.pop(0))
            first_q = casts[0][0]
            casts.clear()

            def first_casts(g, half):
                cols = slice(g * CH, (g + 1) * CH)
                for j in (2 * half, 2 * half + 1):
                    if half == 0:
                        nc.vector.tensor_copy(out=raw_of[first_q][:, j, cols], in_=byt[0][:, j, cols].bitcast(FP8))
                    else:
                        nc.scalar.copy(out=raw_of[first_q][:, j, cols], in_=byt[0][:, j, cols].bitcast(FP8))

            g_pairs = g_bc[:].rearrange("p w (i e) -> p w i e", e=2)
            gsw_pairs = gsw[:].rearrange("p w (i e) -> p w i e", e=2)

            def signed_gain(i):
                nc.gpsimd.tensor_scalar(out=gsw_pairs[:, i, :, 0], in0=g_pairs[:, i, :, 0], scalar1=1.0, scalar2=0.0, op0=MULT, op1=ADD)
                nc.gpsimd.tensor_scalar(out=gsw_pairs[:, i, :, 1], in0=g_pairs[:, i, :, 1], scalar1=-1.0, scalar2=0.0, op0=MULT, op1=ADD)

            def tables_of(i):
                w = names[i]
                lo, hi = tiles_of[w]
                n = hi - lo
                signed_gain(i)
                nc.gpsimd.tensor_tensor(
                    out=rot[w][:, :, 0, :],
                    in0=cos_sb[:, lo:hi, :],
                    in1=g_bc[:, i, :].rearrange("p (o d) -> p o d", o=1).to_broadcast([P, n, HD]),
                    op=MULT,
                )
                nc.gpsimd.tensor_tensor(
                    out=rot[w][:, :, 1, :].rearrange("p j (i e) -> p j i e", e=2),
                    in0=sin_sb[:, lo:hi, :].rearrange("p j (i e) -> p j i e", e=2)[:, :, :, ::-1],
                    in1=gsw[:, i, :].rearrange("p (o i e) -> p o i e", o=1, e=2).to_broadcast([P, n, HD // 2, 2]),
                    op=MULT,
                )

            def first_tables():
                nc.gpsimd.tensor_copy(out=gate[:], in_=raw_of[first_q][:, 1, D - 2 : D])
                tables_of(0)
                tables_of(1)

            def text_tables():
                nc.gpsimd.tensor_copy(out=gate2[:], in_=live[banks[0]][1][:, 0:2])
                tables_of(2)
                tables_of(3)

            state = {"units": 0}
            products = []
            quants = []
            quanted = set()

            def finish(gi, slot):
                left[gi] -= 1
                if left[gi] == 0:
                    quants.append((gi, slot))

            def advance(slot, upto_group):
                while state["units"] < len(units) and (when[state["units"]] <= slot or any(left[gi] > 0 and u[1] == gi for gi in upto_group for u in units[state["units"] :])):
                    gi, g, half = units[state["units"]][1:]
                    kind = groups[gi][0]
                    while casts and casts[0][0] == gi and casts[0][1] <= 2 * half + 1:
                        cast(False)
                    if gi == first_q:
                        first_casts(g, half)
                        if (g, half) == (PASSES - 1, 0):
                            first_tables()
                    product = unit(gi, g, half)
                    state["units"] += 1
                    if product is None:
                        finish(gi, slot)
                    else:
                        products.append((product, gi))
                    if all(u[1] != gi for u in units[state["units"] :]):
                        if kind in weight and bf_groups:
                            load_group(bf_groups.pop(0))
                        if kind == "q" and q_groups:
                            load_group(q_groups.pop(0))

            def product_now(slot):
                product, gi = products.pop(0)
                product()
                finish(gi, slot - QLAG)

            def quant_group(gi):
                for g in range(PASSES):
                    quant(gi, g)
                quanted.add(gi)

            def both_port_work(slot):
                if products:
                    product_now(slot)
                while quants and quants[0][1] + QLAG <= slot:
                    quant_group(quants.pop(0)[0])

            for s in range(len(banks) + DELAY):
                if s < len(banks):
                    gi, m = banks[s]
                    early = groups[gi][0] in bias and m == 0 and gi in quanted and 0 in quanted
                    if early:
                        text_heads(gi)
                    advance(s + PERIOD - 1 - s % PERIOD, (gi, m // 2))
                    while any(p[1] == gi for p in products):
                        product_now(s)
                    while gi not in quanted or m // 2 not in quanted:
                        quant_group(quants.pop(0)[0])
                    if casts and s % 2 == 0:
                        cast(False)
                    if groups[gi][0] in bias and m == 0 and not early:
                        text_heads(gi)
                    bank_a(gi, m)
                    if s == 0:
                        text_tables()
                if s >= DELAY:
                    bank_b(*banks[s - DELAY], lambda: both_port_work(s))
